import numpy as np
import ml_dtypes


def mxq(x, axis, fmt="e4m3"):
    dtype, down = {"e4m3": (ml_dtypes.float8_e4m3fn, 7), "e5m2": (ml_dtypes.float8_e5m2, 14)}[fmt]
    v = np.moveaxis(np.asarray(x, np.float32).astype(ml_dtypes.bfloat16).astype(np.float64), axis, -1)
    blocks = v.reshape(v.shape[:-1] + (-1, 32))
    amax = np.abs(blocks).max(-1, keepdims=True)
    byte = np.maximum(np.where(amax > 0, np.frexp(amax)[1] - 1 + 127, 0) - down, 1)
    scale = np.exp2(byte - 127.0)
    codes = (blocks / scale).astype(np.float32).astype(dtype).astype(np.float64)
    return np.moveaxis((codes * scale).reshape(v.shape), -1, axis)


WIDE = False


def mx_kscale(k):
    if not WIDE:
        return np.ones(k)
    levels = np.array([10, -10, 5, -5, 0])
    if k % 512:
        return np.exp2(np.random.permutation(np.resize(levels, k // 32))).repeat(32)
    a = np.empty((k // 512, 16))
    for p in range(k // 512):
        a[p, :8] = np.random.permutation(np.resize(levels, 8))
        for g in range(8):
            far = levels[np.abs(levels - a[p, g]) >= 10]
            a[p, g + 8] = far[np.random.randint(len(far))]
    return np.exp2(a.ravel()).repeat(32)


BF16 = ml_dtypes.bfloat16


def bf(x):
    return np.asarray(x, np.float32).astype(BF16)


def f64(x):
    return np.asarray(x).astype(np.float64)


B, L, D, H, HD, MINI, NCH, TEXT, OFF = 4, 512, 1024, 16, 64, 64, 4, 64, 128


def rope_table():
    inv_freq = 1.0 / (10000.0 ** (np.arange(0, HD, 2) / HD))
    ang = np.outer(np.arange(L), inv_freq)
    return np.stack([np.cos(ang), np.sin(ang)], axis=-1)


def l2norm(x):
    return x / np.maximum(np.sqrt((x * x).sum(-1, keepdims=True)), 1e-12)


def rope(x, cos, sin):
    c = cos[None, :, None, :]
    s = sin[None, :, None, :]
    xr, xi = x[..., 0::2], x[..., 1::2]
    return np.stack([xr * c - xi * s, xr * s + xi * c], axis=-1).reshape(x.shape)


def draw0():
    s = mx_kscale(D)
    return {"hidden_states": bf(np.random.standard_normal((B, L, D)) * s),
            "freqs_cis": bf(rope_table()),
            "wk_w": bf(np.random.standard_normal((D, D)) / np.sqrt(D) / s[:, None]),
            "wk_b": bf(np.random.standard_normal(D) * 0.1),
            "wv_w": bf(np.random.standard_normal((D, D)) * 0.5 / np.sqrt(D) / s[:, None]),
            "wv_b": bf(np.random.standard_normal(D) * 0.1),
            "ttt_norm_weight": bf(1.0 + 0.1 * np.random.standard_normal((H, HD))),
            "ttt_norm_bias": bf(0.1 * np.random.standard_normal((H, HD)))}


def core(hidden_states, freqs_cis, wk_w, wk_b, wv_w, wv_b, ttt_norm_weight, ttt_norm_bias):
    hq = mxq(f64(hidden_states), 2, "e4m3")
    xk = ((hq @ mxq(f64(wk_w), 0, "e4m3")) + f64(wk_b)).reshape(B, L, H, HD)
    xv = ((hq @ mxq(f64(wv_w), 0, "e4m3")) + f64(wv_b)).reshape(B, L, H, HD)
    fc = f64(freqs_cis)
    xk = rope(l2norm(xk), fc[..., 0], fc[..., 1])
    diff = xv - xk
    mean = diff.mean(axis=-1, keepdims=True)
    std = diff.std(axis=-1, keepdims=True, ddof=1)
    norm = (diff - mean) / (std + 1e-8)
    xv = f64(ttt_norm_weight)[None, None] * norm + f64(ttt_norm_bias)[None, None] + xk
    return xk, xv


def e4m3fn_bytes(y):
    return np.clip(np.asarray(y, np.float64), -448.0, 448.0).astype(np.float32).astype(ml_dtypes.float8_e4m3fn).view(np.uint8)


def e4m3fn_values(b):
    return np.asarray(b, np.uint8).view(ml_dtypes.float8_e4m3fn).astype(np.float64)


def setup_inputs():
    d = draw0()
    x0 = np.asarray(d['hidden_states']).astype(np.float64)
    s = (np.max(np.abs(x0), axis=(0, 1), keepdims=True) / 448.0).astype(np.float32)
    out = {}
    for k, v in d.items():
        if k == 'hidden_states':
            out['hidden_states_bytes'] = e4m3fn_bytes(x0 / s.astype(np.float64))
            out['hidden_states_scale'] = s
        else:
            out[k] = v
    return out


def reference(hidden_states_bytes, hidden_states_scale, freqs_cis, wk_w, wk_b, wv_w, wv_b, ttt_norm_weight, ttt_norm_bias):
    return core(e4m3fn_values(hidden_states_bytes) * hidden_states_scale.astype(np.float64), freqs_cis, wk_w, wk_b, wv_w, wv_b, ttt_norm_weight, ttt_norm_bias)

@@ -1,0 +1,508 @@
+from contextlib import ExitStack
+
+import concourse.mybir as mybir
+from concourse.masks import make_identity
+
+F32 = mybir.dt.float32
+BF16 = mybir.dt.bfloat16
+U8 = mybir.dt.uint8
+U32 = mybir.dt.uint32
+FP8 = mybir.dt.float8_e4m3fn
+FP8X4 = mybir.dt.float8_e4m3fn_x4
+ALU = mybir.AluOpType
+ACT = mybir.ActivationFunctionType
+AX = mybir.AxisListType
+
+B, L, D, H, HD = 4, 512, 1024, 16, 64
+P = 128
+UH = 8
+CD = 16
+FLOPS = 2 * (B * L) * D * (2 * D)
+
+
+def tile_tttwrapper_pa_kernel(
+    tc,
+    hidden_states_bytes,
+    hidden_states_scale,
+    freqs_cis,
+    wk_w,
+    wk_b,
+    wv_w,
+    wv_b,
+    ttt_norm_weight,
+    ttt_norm_bias,
+    out_0,
+    out_1,
+):
+    nc = tc.nc
+    with ExitStack() as ctx:
+        const = ctx.enter_context(tc.tile_pool(name="const", bufs=1))
+        codes = ctx.enter_context(tc.tile_pool(name="codes", bufs=1))
+        bytes_pool = ctx.enter_context(tc.tile_pool(name="bytes_pool", bufs=2))
+        wraw_pool = ctx.enter_context(tc.tile_pool(name="wraw_pool", bufs=2))
+        wgrp_pool = ctx.enter_context(tc.tile_pool(name="wgrp_pool", bufs=4))
+        xb_pool = ctx.enter_context(tc.tile_pool(name="xb_pool", bufs=2))
+        hgrp_pool = ctx.enter_context(tc.tile_pool(name="hgrp_pool", bufs=2))
+        xrep_pool = ctx.enter_context(tc.tile_pool(name="xrep_pool", bufs=2))
+        chan = ctx.enter_context(tc.tile_pool(name="chan", bufs=9))
+        sq_pool = ctx.enter_context(tc.tile_pool(name="sq_pool", bufs=5))
+        xk_pool = ctx.enter_context(tc.tile_pool(name="xk_pool", bufs=6))
+        y_pool = ctx.enter_context(tc.tile_pool(name="y_pool", bufs=6))
+        bxk_pool = ctx.enter_context(tc.tile_pool(name="bxk_pool", bufs=1))
+        stat = ctx.enter_context(tc.tile_pool(name="stat", bufs=4))
+        ps_mx = ctx.enter_context(tc.psum_pool(name="ps_mx", bufs=2))
+        ps_rk = ctx.enter_context(tc.psum_pool(name="ps_rk", bufs=2))
+        ps_v0 = ctx.enter_context(tc.psum_pool(name="ps_v0", bufs=2))
+        ps_st = ctx.enter_context(tc.psum_pool(name="ps_st", bufs=1))
+        ps_xt = ctx.enter_context(tc.psum_pool(name="ps_xt", bufs=1))
+        ctx.enter_context(tc.manual_schedule())
+
+        weights = (wk_w, wv_w)
+
+        wraw = {}
+
+        def load_weights(mat, hf):
+            raw = wraw_pool.tile([P, 2, 4, 512], BF16, name="wraw%d" % mat, tag="wraw%d" % mat)
+            for g in range(2):
+                nc.sync.dma_start(
+                    out=raw[:, g, :, :],
+                    in_=weights[mat][512 * g : 512 * (g + 1), 512 * hf : 512 * (hf + 1)].rearrange(
+                        "(p j) n -> p j n", j=4
+                    ),
+                )
+            wraw[(mat, hf)] = raw
+
+        hbytes = {}
+
+        def load_bytes(b):
+            hb = bytes_pool.tile([P, 4, D], U8, name="hbytes", tag="hbytes")
+            nc.sync.dma_start(out=hb[:], in_=hidden_states_bytes[b].rearrange("(t p) k -> p t k", p=P))
+            hbytes[b] = hb
+
+        fc = const.tile([P, 4, 64], BF16, name="fc")
+        nc.scalar.dma_start(out=fc[:], in_=freqs_cis.rearrange("(t p) j c -> p t (j c)", p=P))
+        brow = const.tile([P, P], BF16, name="brow")
+        nc.vector.memset(brow[:], 0.0)
+        for m, vec in enumerate((wk_b, wv_b)):
+            for f in range(2):
+                nc.scalar.dma_start(
+                    out=brow[8 * m + 4 * f : 8 * m + 4 * f + 4, :].rearrange("r (h d) -> r h d", h=UH),
+                    in_=vec.rearrange("(f h i d) -> f i h d", f=2, h=UH, i=4)[f],
+                )
+        sc = const.tile([P, D], F32, name="sc")
+        nc.scalar.dma_start(out=sc[:], in_=hidden_states_scale.rearrange("a b k -> (a b k)").partition_broadcast(P))
+        load_bytes(0)
+        load_weights(0, 0)
+        load_weights(1, 0)
+        w_b = const.tile([P, D], BF16, name="w_b")
+        nc.scalar.dma_start(out=w_b[:], in_=ttt_norm_weight.rearrange("h d -> (h d)").partition_broadcast(P))
+        b_b = const.tile([P, D], BF16, name="b_b")
+        nc.scalar.dma_start(out=b_b[:], in_=ttt_norm_bias.rearrange("h d -> (h d)").partition_broadcast(P))
+        load_bytes(1)
+        load_weights(0, 1)
+        load_weights(1, 1)
+        load_bytes(2)
+        load_bytes(3)
+
+        one = const.tile([P, 1], F32, name="one")
+        nc.vector.memset(one[:], 1.0)
+        one2 = const.tile([P, 1], F32, name="one2")
+        nc.scalar.activation(out=one2[:], in_=one[:], func=ACT.Sqrt)
+
+        ident = const.tile([P, P], F32, name="ident")
+        make_identity(nc, ident[:])
+        pswap = const.tile([P, P], F32, name="pswap")
+        iv = ident[:].rearrange("p (j e) -> p j e", e=2)
+        sv = pswap[:].rearrange("p (j e) -> p j e", e=2)
+        nc.gpsimd.tensor_copy(out=sv[:, :, 0:1], in_=iv[:, :, 1:2])
+        nc.gpsimd.tensor_copy(out=sv[:, :, 1:2], in_=iv[:, :, 0:1])
+
+        def turn_op(dst, src, perm, first, last):
+            return lambda: nc.tensor.matmul(out=dst, lhsT=src, rhs=perm[:], is_transpose=True, start=first, stop=last)
+
+        ftok = const.tile([P, 4, 2, HD], F32, name="ftok")
+        fcv = fc[:].rearrange("p t (j c) -> p t j c", c=2)
+        fv = ftok[:].rearrange("p t c (j e) -> p t c j e", e=2)
+        for e in range(2):
+            nc.vector.tensor_copy(out=fv[:, :, 0, :, e], in_=fcv[:, :, :, 0])
+            nc.vector.tensor_scalar(
+                out=fv[:, :, 1, :, e], in0=fcv[:, :, :, 1], scalar1=(1.0 if e == 0 else -1.0), scalar2=None, op0=ALU.mult
+            )
+        tabs = [const.tile([P, 4, L], BF16, name=nm) for nm in ("cos_t", "sin_t")]
+        xreps = {}
+
+        def table_a(i):
+            for c in range(2):
+                xrep = xrep_pool.tile([P, 4, UH, CD], F32, name="xrep", tag="xrep")
+                nc.vector.tensor_copy(
+                    out=xrep[:], in_=ftok[:, :, c, CD * i : CD * (i + 1)].unsqueeze(2).to_broadcast([P, 4, UH, CD])
+                )
+                xreps[(i, c)] = xrep
+
+        def table_b(i):
+            for c, pool, tg in ((0, ps_rk, "rk"), (1, ps_v0, "v0")):
+                pc = pool.tile([P, L], F32, name="pc", tag=tg)
+                for t in range(4):
+                    turn_op(pc[:, t * P : (t + 1) * P], xreps[(i, c)][:, t, :, :].rearrange("p h d -> p (h d)"), ident, True, True)()
+                nc.scalar.copy(out=tabs[c][:, i, :], in_=pc[:])
+
+        table_a(0)
+        table_b(0)
+
+        browf = const.tile([P, P], F32, name="browf")
+        nc.vector.tensor_copy(out=browf[:], in_=brow[:])
+        pb = ps_st.tile([P, P], F32, name="pb", tag="st")
+        nc.tensor.transpose(pb[:], browf[:], ident[:])
+        bias_t = const.tile([P, 16], F32, name="bias_t")
+        nc.scalar.copy(out=bias_t[:], in_=pb[:, 0:16])
+
+        wcodes = [codes.tile([P, 8, 2, P], U32, name="wcodes%d" % m, align_bytes=64) for m in range(2)]
+        wscales = [codes.tile([P, 8, 2, P], U8, name="wscales%d" % m, align_bytes=64) for m in range(2)]
+        hcodes = codes.tile([P, 2, B * L], U32, name="hcodes", align_bytes=64)
+        hscales = codes.tile([P, 2, B * L], U8, name="hscales", align_bytes=64)
+
+        wgrp = {}
+
+        def copy_chunk(mat, c):
+            hf, i = divmod(c, 4)
+            grp = wgrp_pool.tile([P, 2, P, 4], BF16, name="wgrp", tag="wgrp", align_bytes=64)
+            for g in range(2):
+                src = wraw[(mat, hf)][:, g, :, :].rearrange("p j (h i d) -> p i h d j", h=UH, i=4)[:, i]
+                dst = grp[:, g, :, :].rearrange("p (h d) j -> p h d j", h=UH)
+                if mat == 0:
+                    nc.vector.tensor_copy(out=dst, in_=src)
+                else:
+                    nc.scalar.copy(out=dst, in_=src)
+            wgrp[(mat, c)] = grp
+
+        def quant_chunk(mat, c):
+            nc.vector.quantize_mx(
+                out=wcodes[mat][:, c, :, :].rearrange("p g n -> p (g n)").bitcast(FP8X4),
+                scales=wscales[mat][:, c, :, :].rearrange("p g n -> p (g n)"),
+                in_=wgrp[(mat, c)][:].rearrange("p g n j -> p (g n j)"),
+            )
+
+        hgrp = {}
+        xbs = {}
+
+        def widen(b, t):
+            if t == 0:
+                hgrp[b] = hgrp_pool.tile([P, 2, L, 4], BF16, name="hgrp", tag="hgrp", align_bytes=64)
+            xb = xb_pool.tile([P, D], BF16, name="xb", tag="xb", align_bytes=64)
+            nc.vector.tensor_tensor(out=xb[:], in0=hbytes[b][:, t, :].bitcast(FP8), in1=sc[:], op=ALU.mult)
+            xbs[(b, t)] = xb
+
+        xts = {}
+
+        def turn(b, t):
+            words = xbs[(b, t)][:].bitcast(F32)
+            xt = ps_xt.tile([P, 2, 2, P], F32, name="xt", tag="xt")
+            xts[(b, t)] = xt
+            return [
+                turn_op(xt[:, g, u, :], words[:, 256 * g + u : 256 * (g + 1) : 2], ident, True, True)
+                for g in range(2)
+                for u in range(2)
+            ]
+
+        def evacuate(b, t):
+            nc.scalar.copy(
+                out=hgrp[b][:].bitcast(F32)[:, :, t * P : (t + 1) * P, :],
+                in_=xts[(b, t)][:].rearrange("p g u r -> p g r u"),
+            )
+
+        def quant_hidden(b, half):
+            for g in range(2):
+                tok = slice(b * L + half * 256, b * L + (half + 1) * 256)
+                nc.vector.quantize_mx(
+                    out=hcodes[:, g, tok].bitcast(FP8X4),
+                    scales=hscales[:, g, tok],
+                    in_=hgrp[b][:, g, half * 256 : (half + 1) * 256, :].rearrange("p r j -> p (r j)"),
+                )
+
+        work = {}
+
+        def matmuls(n, i):
+            b, hf = divmod(n, 2)
+            tok = slice(b * L, (b + 1) * L)
+            c = 4 * hf + i
+            if i == 0:
+                work[n] = {"a": [], "bb": [], "sq": [], "vt": [], "xk": [], "y": [], "pk": [], "pv": [], "rk": [], "v0": []}
+            w = work[n]
+            for mat, key in ((0, "pk"), (1, "pv")):
+                acc = ps_mx.tile([P, L], F32, name=key, tag=key, bufs=1)
+                for g in range(2):
+                    nc.tensor.matmul_mx(
+                        out=acc[:],
+                        lhsT=wcodes[mat][:, c, g, :].bitcast(FP8X4),
+                        lhsT_scale=wscales[mat][:, c, g, :],
+                        rhs=hcodes[:, g, tok].bitcast(FP8X4),
+                        rhs_scale=hscales[:, g, tok],
+                        start=(g == 0),
+                        stop=(g == 1),
+                    )
+                w[key].append(acc)
+
+        def scalar_out(n, i):
+            ct = 4 * (n % 2) + i
+            w = work[n]
+            sq = sq_pool.tile([P, L], F32, name="sq", tag="sq")
+            nc.scalar.activation(out=sq[:], in_=w["pk"][i][:], func=ACT.Square, bias=bias_t[:, ct : ct + 1], scale=1.0)
+            vt = chan.tile([P, L], F32, name="vt", tag="vt")
+            nc.scalar.activation(
+                out=vt[:], in_=w["pv"][i][:], func=ACT.Identity, bias=bias_t[:, 8 + ct : 9 + ct], scale=1.0
+            )
+            w["sq"].append(sq)
+            w["vt"].append(vt)
+
+        def vector_out(n, i):
+            ct = 4 * (n % 2) + i
+            w = work[n]
+            for key, c in (("a", 0), ("bb", 1)):
+                prod = chan.tile([P, L], F32, name=key, tag=key)
+                nc.vector.scalar_tensor_tensor(
+                    out=prod[:], in0=w["pk"][i][:], scalar=bias_t[:, ct : ct + 1], in1=tabs[c][:, i, :], op0=ALU.add, op1=ALU.mult
+                )
+                w[key].append(prod)
+
+        def fold(n, key):
+            w = work[n]
+            st = ps_st.tile([P, 4 * P], F32, name="st", tag="st")
+            w["st" + key] = st
+            return [
+                turn_op(st[:, t * P : (t + 1) * P], w[key][i][:, t * P : (t + 1) * P], ident, i == 0, i == 3)
+                for t in range(4)
+                for i in range(4)
+            ]
+
+        def head_sum(n, key, name):
+            out = stat.tile([P, 32], F32, name=name, tag=name)
+            nc.vector.tensor_reduce(
+                out=out[:], in_=work[n]["st" + key][:].rearrange("p (c d) -> p c d", d=CD), axis=AX.X, op=ALU.add
+            )
+            return out
+
+        def norm_a(n):
+            ss = head_sum(n, "sq", "ss")
+            nc.vector.tensor_scalar(out=ss[:], in0=ss[:], scalar1=1e-24, scalar2=None, op0=ALU.max)
+            work[n]["ss"] = ss
+
+        def norm_b(n):
+            w = work[n]
+            rho = stat.tile([P, 32], F32, name="rho", tag="rho")
+            nc.scalar.activation(out=rho[:], in_=w["ss"][:], func=ACT.Sqrt)
+            w["rho"] = rho
+
+        def norm_c(n):
+            w = work[n]
+            r = stat.tile([P, 32], F32, name="r", tag="r")
+            nc.vector.reciprocal(out=r[:], in_=w["rho"][:])
+            w["r"] = r
+            w["sxk"] = stat.tile([P, 32], F32, name="sxk", tag="sxk")
+            w["vs"] = stat.tile([P, 32], F32, name="vs", tag="vs")
+            w["negm"] = stat.tile([P, 32], F32, name="negm", tag="negm")
+
+        def mean_a(n):
+            mv = head_sum(n, "vt", "mv")
+            nc.vector.tensor_scalar(out=mv[:], in0=mv[:], scalar1=1.0 / HD, scalar2=None, op0=ALU.mult)
+            work[n]["mv"] = mv
+
+        def turn_back(n, t):
+            w = work[n]
+            ts = slice(t * P, (t + 1) * P)
+            rk = ps_rk.tile([P, 512], F32, name="rk", tag="rk")
+            v0 = ps_v0.tile([P, 512], F32, name="v0", tag="v0")
+            w["rk"].append(rk)
+            w["v0"].append(v0)
+            ops = []
+            for i in range(4):
+                cs = slice(i * P, (i + 1) * P)
+                ops.append(turn_op(rk[:, cs], w["a"][i][:, ts], ident, True, False))
+                ops.append(turn_op(rk[:, cs], w["bb"][i][:, ts], pswap, False, True))
+            for i in range(4):
+                cs = slice(i * P, (i + 1) * P)
+                ops.append(turn_op(v0[:, cs], w["vt"][i][:, ts], ident, True, True))
+            return ops
+
+        def keys(n, t):
+            b, hf = divmod(n, 2)
+            w = work[n]
+            rkv = w["rk"][t][:].rearrange("p (i h d) -> p h i d", i=4, h=UH)
+            xk = xk_pool.tile([P, 512], F32, name="xk", tag="xk")
+            xkv = xk[:].rearrange("p (h i d) -> p h i d", h=UH, i=4)
+            for h in range(UH):
+                c = t * 8 + h
+                nc.scalar.activation(
+                    out=xkv[:, h], in_=rkv[:, h], func=ACT.Copy, scale=w["r"][:, c : c + 1], accum_out=w["sxk"][:, c : c + 1]
+                )
+            nc.sync.dma_start(
+                out=out_0[b, t * P : (t + 1) * P, 8 * hf : 8 * hf + 8, :].rearrange("l h d -> l (h d)"), in_=xk[:]
+            )
+            w["xk"].append(xk)
+
+        def difference(n, t):
+            w = work[n]
+            y = y_pool.tile([P, 512], F32, name="y", tag="y")
+            nc.vector.tensor_tensor(
+                out=y[:].rearrange("p (h i d) -> p h i d", h=UH, i=4),
+                in0=w["v0"][t][:].rearrange("p (i h d) -> p h i d", i=4, h=UH),
+                in1=w["xk"][t][:].rearrange("p (h i d) -> p h i d", h=UH, i=4),
+                op=ALU.subtract,
+            )
+            cs = slice(t * 8, (t + 1) * 8)
+            nc.vector.scalar_tensor_tensor(
+                out=w["negm"][:, cs], in0=w["sxk"][:, cs], scalar=1.0 / HD, in1=w["mv"][:, cs], op0=ALU.mult, op1=ALU.subtract
+            )
+            w["y"].append(y)
+
+        def squares(n, t):
+            w = work[n]
+            junk = stat.tile([P, HD], BF16, name="junk", tag="junk")
+            for h in range(UH):
+                c = t * 8 + h
+                hs = slice(h * HD, (h + 1) * HD)
+                nc.scalar.activation(
+                    out=junk[:],
+                    in_=w["y"][t][:, hs],
+                    func=ACT.Square,
+                    bias=w["negm"][:, c : c + 1],
+                    scale=1.0,
+                    accum_out=w["vs"][:, c : c + 1],
+                )
+
+        def spread_a(n):
+            w = work[n]
+            var = stat.tile([P, 32], F32, name="var", tag="var")
+            nc.vector.tensor_scalar(
+                out=var[:], in0=w["vs"][:], scalar1=1.0 / (HD - 1), scalar2=1e-30, op0=ALU.mult, op1=ALU.max
+            )
+            w["var"] = var
+
+        def spread_b(n):
+            w = work[n]
+            std = stat.tile([P, 32], F32, name="std", tag="std")
+            nc.scalar.activation(out=std[:], in_=w["var"][:], func=ACT.Sqrt)
+            w["std"] = std
+
+        def spread_c(n):
+            w = work[n]
+            sg = stat.tile([P, 32], F32, name="sg", tag="sg")
+            nc.vector.tensor_scalar(out=sg[:], in0=w["std"][:], scalar1=1e-8, scalar2=None, op0=ALU.add)
+            q = stat.tile([P, 32], F32, name="q", tag="q")
+            nc.vector.reciprocal(out=q[:], in_=sg[:])
+            w["q"] = q
+
+        bxks = {}
+
+        def shifted_keys(n, t):
+            hf = n % 2
+            bxk = bxk_pool.tile([P, 512], F32, name="bxk", tag="bxk")
+            nc.gpsimd.tensor_tensor(out=bxk[:], in0=work[n]["xk"][t][:], in1=b_b[:, 512 * hf : 512 * (hf + 1)], op=ALU.add)
+            bxks[(n, t)] = bxk
+
+        def target(n, t):
+            b, hf = divmod(n, 2)
+            w = work[n]
+            y = w["y"][t]
+            bxk = bxks[(n, t)]
+            for h in range(UH):
+                c = t * 8 + h
+                hs = slice(h * HD, (h + 1) * HD)
+                ws = slice(512 * hf + h * HD, 512 * hf + (h + 1) * HD)
+                nc.vector.scalar_tensor_tensor(
+                    out=y[:, hs], in0=y[:, hs], scalar=w["negm"][:, c : c + 1], in1=w_b[:, ws], op0=ALU.add, op1=ALU.mult
+                )
+            for h in range(UH):
+                c = t * 8 + h
+                hs = slice(h * HD, (h + 1) * HD)
+                nc.vector.scalar_tensor_tensor(
+                    out=y[:, hs], in0=y[:, hs], scalar=w["q"][:, c : c + 1], in1=bxk[:, hs], op0=ALU.mult, op1=ALU.add
+                )
+            nc.sync.dma_start(
+                out=out_1[b, t * P : (t + 1) * P, 8 * hf : 8 * hf + 8, :].rearrange("l h d -> l (h d)"), in_=y[:]
+            )
+
+        def run(ops):
+            for op in ops:
+                op()
+
+        widen(0, 0)
+        widen(0, 1)
+        run(turn(0, 0))
+        evacuate(0, 0)
+        widen(0, 2)
+        run(turn(0, 1))
+        evacuate(0, 1)
+        widen(0, 3)
+        run(turn(0, 2))
+        evacuate(0, 2)
+        run(turn(0, 3))
+        evacuate(0, 3)
+        copy_chunk(0, 0)
+        quant_hidden(0, 0)
+        quant_chunk(0, 0)
+        copy_chunk(0, 1)
+        quant_hidden(0, 1)
+        copy_chunk(1, 0)
+        copy_chunk(1, 1)
+        quant_chunk(1, 0)
+
+        NSTEP = 32
+
+        def at(k):
+            return divmod(k, 4) if 0 <= k < NSTEP else None
+
+        def unit_at(k):
+            return k // 4 if (0 <= k < NSTEP and k % 4 == 0) else None
+
+        for s in range(NSTEP + 11):
+            if unit_at(s - 5) is not None:
+                norm_c(unit_at(s - 5))
+            if unit_at(s - 10) is not None:
+                spread_a(unit_at(s - 10))
+                spread_b(unit_at(s - 10))
+            if at(s - 5):
+                run(turn_back(*at(s - 5)))
+            if unit_at(s - 4) is not None:
+                run(fold(unit_at(s - 4), "sq"))
+            if unit_at(s - 5) is not None:
+                run(fold(unit_at(s - 5), "vt"))
+            if 1 <= s <= 12:
+                run(turn(1 + (s - 1) // 4, (s - 1) % 4))
+            if at(s - 6):
+                difference(*at(s - 6))
+            if at(s - 5):
+                keys(*at(s - 5))
+            if unit_at(s - 10) is not None:
+                spread_c(unit_at(s - 10))
+            if at(s - 10):
+                target(*at(s - 10))
+            if at(s - 9):
+                shifted_keys(*at(s - 9))
+            if 1 <= s <= 12:
+                evacuate(1 + (s - 1) // 4, (s - 1) % 4)
+            if 0 <= s + 1 < 8:
+                quant_chunk(0, s + 1)
+                quant_chunk(1, s + 1)
+            if 0 <= s + 2 < 8:
+                copy_chunk(0, s + 2)
+            if 2 <= s <= 13 and s % 2 == 1:
+                quant_hidden(1 + (s - 2) // 4, ((s - 2) % 4) // 2)
+            if 0 <= s <= 11:
+                widen(1 + s // 4, s % 4)
+            if s + 1 < 4:
+                table_a(s + 1)
+            if at(s):
+                matmuls(*at(s))
+                scalar_out(*at(s))
+                vector_out(*at(s))
+            if at(s - 6):
+                squares(*at(s - 6))
+            if 0 <= s + 2 < 8:
+                copy_chunk(1, s + 2)
+            if s + 1 < 4:
+                table_b(s + 1)
+            if unit_at(s - 4) is not None:
+                norm_a(unit_at(s - 4))
+                norm_b(unit_at(s - 4))
+            if unit_at(s - 5) is not None:
+                mean_a(unit_at(s - 5))

@@ -47,7 +47,7 @@ def tile_tttwrapper_pa_kernel(
         chan = ctx.enter_context(tc.tile_pool(name="chan", bufs=9))
         sq_pool = ctx.enter_context(tc.tile_pool(name="sq_pool", bufs=5))
         xk_pool = ctx.enter_context(tc.tile_pool(name="xk_pool", bufs=6))
-        y_pool = ctx.enter_context(tc.tile_pool(name="y_pool", bufs=6))
+        y_pool = ctx.enter_context(tc.tile_pool(name="y_pool", bufs=7))
         bxk_pool = ctx.enter_context(tc.tile_pool(name="bxk_pool", bufs=1))
         stat = ctx.enter_context(tc.tile_pool(name="stat", bufs=4))
         ps_mx = ctx.enter_context(tc.psum_pool(name="ps_mx", bufs=2))
@@ -356,12 +356,12 @@ def tile_tttwrapper_pa_kernel(
 
         def squares(n, t):
             w = work[n]
-            junk = stat.tile([P, HD], BF16, name="junk", tag="junk")
+            junk = stat.tile([P, UH * HD], BF16, name="junk", tag="junk")
             for h in range(UH):
                 c = t * 8 + h
                 hs = slice(h * HD, (h + 1) * HD)
                 nc.scalar.activation(
-                    out=junk[:],
+                    out=junk[:, hs],
                     in_=w["y"][t][:, hs],
                     func=ACT.Square,
                     bias=w["negm"][:, c : c + 1],
@@ -399,24 +399,27 @@ def tile_tttwrapper_pa_kernel(
             nc.gpsimd.tensor_tensor(out=bxk[:], in0=work[n]["xk"][t][:], in1=b_b[:, 512 * hf : 512 * (hf + 1)], op=ALU.add)
             bxks[(n, t)] = bxk
 
+        def by_head(n, t, key):
+            return work[n][key][:, t * 8 : (t + 1) * 8].unsqueeze(2).to_broadcast([P, UH, HD])
+
+        def centre(n, t):
+            yv = work[n]["y"][t][:].rearrange("p (h d) -> p h d", h=UH)
+            nc.gpsimd.tensor_tensor(out=yv, in0=yv, in1=by_head(n, t, "negm"), op=ALU.add)
+
+        def weigh(n, t):
+            hf = n % 2
+            y = work[n]["y"][t]
+            nc.vector.tensor_tensor(out=y[:], in0=y[:], in1=w_b[:, 512 * hf : 512 * (hf + 1)], op=ALU.mult)
+
+        def scale(n, t):
+            yv = work[n]["y"][t][:].rearrange("p (h d) -> p h d", h=UH)
+            nc.vector.tensor_tensor(out=yv, in0=yv, in1=by_head(n, t, "q"), op=ALU.mult)
+
         def target(n, t):
             b, hf = divmod(n, 2)
             w = work[n]
             y = w["y"][t]
-            bxk = bxks[(n, t)]
-            for h in range(UH):
-                c = t * 8 + h
-                hs = slice(h * HD, (h + 1) * HD)
-                ws = slice(512 * hf + h * HD, 512 * hf + (h + 1) * HD)
-                nc.vector.scalar_tensor_tensor(
-                    out=y[:, hs], in0=y[:, hs], scalar=w["negm"][:, c : c + 1], in1=w_b[:, ws], op0=ALU.add, op1=ALU.mult
-                )
-            for h in range(UH):
-                c = t * 8 + h
-                hs = slice(h * HD, (h + 1) * HD)
-                nc.vector.scalar_tensor_tensor(
-                    out=y[:, hs], in0=y[:, hs], scalar=w["q"][:, c : c + 1], in1=bxk[:, hs], op0=ALU.mult, op1=ALU.add
-                )
+            nc.vector.tensor_tensor(out=y[:], in0=y[:], in1=bxks[(n, t)][:], op=ALU.add)
             nc.sync.dma_start(
                 out=out_1[b, t * P : (t + 1) * P, 8 * hf : 8 * hf + 8, :].rearrange("l h d -> l (h d)"), in_=y[:]
             )
@@ -475,9 +478,15 @@ def tile_tttwrapper_pa_kernel(
             if unit_at(s - 10) is not None:
                 spread_c(unit_at(s - 10))
             if at(s - 10):
+                scale(*at(s - 10))
+            if at(s - 9):
+                weigh(*at(s - 9))
+            if at(s - 10):
                 target(*at(s - 10))
             if at(s - 9):
                 shifted_keys(*at(s - 9))
+            if at(s - 7):
+                centre(*at(s - 7))
             if 1 <= s <= 12:
                 evacuate(1 + (s - 1) // 4, (s - 1) % 4)
             if 0 <= s + 1 < 8:

@@ -117,6 +117,9 @@ def tile_tttwrapper_pa_kernel(
         nc.gpsimd.tensor_copy(out=sv[:, :, 0:1], in_=iv[:, :, 1:2])
         nc.gpsimd.tensor_copy(out=sv[:, :, 1:2], in_=iv[:, :, 0:1])
 
+        negi = const.tile([P, P], F32, name="negi")
+        nc.gpsimd.tensor_scalar(out=negi[:], in0=ident[:], scalar1=-1.0, scalar2=0.0, op0=ALU.mult, op1=ALU.add)
+
         def turn_op(dst, src, perm, first, last):
             return lambda: nc.tensor.matmul(out=dst, lhsT=src, rhs=perm[:], is_transpose=True, start=first, stop=last)
 
@@ -310,17 +313,30 @@ def tile_tttwrapper_pa_kernel(
             w = work[n]
             ts = slice(t * P, (t + 1) * P)
             rk = ps_rk.tile([P, 512], F32, name="rk", tag="rk")
-            v0 = ps_v0.tile([P, 512], F32, name="v0", tag="v0")
             w["rk"].append(rk)
-            w["v0"].append(v0)
             ops = []
             for i in range(4):
                 cs = slice(i * P, (i + 1) * P)
                 ops.append(turn_op(rk[:, cs], w["a"][i][:, ts], ident, True, False))
                 ops.append(turn_op(rk[:, cs], w["bb"][i][:, ts], pswap, False, True))
+            return ops
+
+        def subtract(n, t):
+            w = work[n]
+            ts = slice(t * P, (t + 1) * P)
+            v0 = ps_v0.tile([P, 512], F32, name="v0", tag="v0")
+            w["v0"].append(v0)
+            ops = [
+                lambda: nc.tensor.matmul(
+                    out=v0[:].rearrange("p (i h d) -> p i h d", i=4, h=UH),
+                    lhsT=negi[:],
+                    rhs=w["xk"][t][:].rearrange("p (h i d) -> p i h d", h=UH, i=4),
+                    start=True,
+                    stop=False,
+                )
+            ]
             for i in range(4):
-                cs = slice(i * P, (i + 1) * P)
-                ops.append(turn_op(v0[:, cs], w["vt"][i][:, ts], ident, True, True))
+                ops.append(turn_op(v0[:, i * P : (i + 1) * P], w["vt"][i][:, ts], ident, False, i == 3))
             return ops
 
         def keys(n, t):
@@ -339,18 +355,21 @@ def tile_tttwrapper_pa_kernel(
             )
             w["xk"].append(xk)
 
+        def mean(n, t):
+            w = work[n]
+            cs = slice(t * 8, (t + 1) * 8)
+            nc.vector.scalar_tensor_tensor(
+                out=w["negm"][:, cs], in0=w["sxk"][:, cs], scalar=1.0 / HD, in1=w["mv"][:, cs], op0=ALU.mult, op1=ALU.subtract
+            )
+
         def difference(n, t):
             w = work[n]
             y = y_pool.tile([P, 512], F32, name="y", tag="y")
             nc.vector.tensor_tensor(
                 out=y[:].rearrange("p (h i d) -> p h i d", h=UH, i=4),
                 in0=w["v0"][t][:].rearrange("p (i h d) -> p h i d", i=4, h=UH),
-                in1=w["xk"][t][:].rearrange("p (h i d) -> p h i d", h=UH, i=4),
-                op=ALU.subtract,
-            )
-            cs = slice(t * 8, (t + 1) * 8)
-            nc.vector.scalar_tensor_tensor(
-                out=w["negm"][:, cs], in0=w["sxk"][:, cs], scalar=1.0 / HD, in1=w["mv"][:, cs], op0=ALU.mult, op1=ALU.subtract
+                in1=w["negm"][:, t * 8 : (t + 1) * 8].unsqueeze(2).unsqueeze(3).to_broadcast([P, UH, 4, CD]),
+                op=ALU.add,
             )
             w["y"].append(y)
 
@@ -364,8 +383,6 @@ def tile_tttwrapper_pa_kernel(
                     out=junk[:, hs],
                     in_=w["y"][t][:, hs],
                     func=ACT.Square,
-                    bias=w["negm"][:, c : c + 1],
-                    scale=1.0,
                     accum_out=w["vs"][:, c : c + 1],
                 )
 
@@ -401,10 +418,6 @@ def tile_tttwrapper_pa_kernel(
 
         def by_head(n, t, key):
             return work[n][key][:, t * 8 : (t + 1) * 8].unsqueeze(2).to_broadcast([P, UH, HD])
-
-        def centre(n, t):
-            yv = work[n]["y"][t][:].rearrange("p (h d) -> p h d", h=UH)
-            nc.gpsimd.tensor_tensor(out=yv, in0=yv, in1=by_head(n, t, "negm"), op=ALU.add)
 
         def weigh(n, t):
             hf = n % 2
@@ -463,6 +476,8 @@ def tile_tttwrapper_pa_kernel(
             if unit_at(s - 10) is not None:
                 spread_a(unit_at(s - 10))
                 spread_b(unit_at(s - 10))
+            if at(s - 6):
+                run(subtract(*at(s - 6)))
             if at(s - 5):
                 run(turn_back(*at(s - 5)))
             if unit_at(s - 4) is not None:
@@ -472,21 +487,21 @@ def tile_tttwrapper_pa_kernel(
             if 1 <= s <= 12:
                 run(turn(1 + (s - 1) // 4, (s - 1) % 4))
             if at(s - 6):
-                difference(*at(s - 6))
+                mean(*at(s - 6))
+            if at(s - 9):
+                weigh(*at(s - 9))
             if at(s - 5):
                 keys(*at(s - 5))
             if unit_at(s - 10) is not None:
                 spread_c(unit_at(s - 10))
             if at(s - 10):
                 scale(*at(s - 10))
-            if at(s - 9):
-                weigh(*at(s - 9))
+            if at(s - 6):
+                difference(*at(s - 6))
             if at(s - 10):
                 target(*at(s - 10))
             if at(s - 9):
                 shifted_keys(*at(s - 9))
-            if at(s - 7):
-                centre(*at(s - 7))
             if 1 <= s <= 12:
                 evacuate(1 + (s - 1) // 4, (s - 1) % 4)
             if 0 <= s + 1 < 8:

@@ -48,7 +48,7 @@ def tile_tttwrapper_pa_kernel(
         sq_pool = ctx.enter_context(tc.tile_pool(name="sq_pool", bufs=5))
         xk_pool = ctx.enter_context(tc.tile_pool(name="xk_pool", bufs=6))
         y_pool = ctx.enter_context(tc.tile_pool(name="y_pool", bufs=7))
-        bxk_pool = ctx.enter_context(tc.tile_pool(name="bxk_pool", bufs=1))
+        bxk_pool = ctx.enter_context(tc.tile_pool(name="bxk_pool", bufs=2))
         stat = ctx.enter_context(tc.tile_pool(name="stat", bufs=4))
         ps_mx = ctx.enter_context(tc.psum_pool(name="ps_mx", bufs=2))
         ps_rk = ctx.enter_context(tc.psum_pool(name="ps_rk", bufs=2))
@@ -284,10 +284,12 @@ def tile_tttwrapper_pa_kernel(
             )
             return out
 
+        def norm_sum(n):
+            work[n]["ss"] = head_sum(n, "sq", "ss")
+
         def norm_a(n):
-            ss = head_sum(n, "sq", "ss")
+            ss = work[n]["ss"]
             nc.vector.tensor_scalar(out=ss[:], in0=ss[:], scalar1=1e-24, scalar2=None, op0=ALU.max)
-            work[n]["ss"] = ss
 
         def norm_b(n):
             w = work[n]
@@ -304,10 +306,12 @@ def tile_tttwrapper_pa_kernel(
             w["vs"] = stat.tile([P, 32], F32, name="vs", tag="vs")
             w["negm"] = stat.tile([P, 32], F32, name="negm", tag="negm")
 
+        def mean_sum(n):
+            work[n]["mv"] = head_sum(n, "vt", "mv")
+
         def mean_a(n):
-            mv = head_sum(n, "vt", "mv")
+            mv = work[n]["mv"]
             nc.vector.tensor_scalar(out=mv[:], in0=mv[:], scalar1=1.0 / HD, scalar2=None, op0=ALU.mult)
-            work[n]["mv"] = mv
 
         def turn_back(n, t):
             w = work[n]
@@ -386,27 +390,23 @@ def tile_tttwrapper_pa_kernel(
                     accum_out=w["vs"][:, c : c + 1],
                 )
 
-        def spread_a(n):
+        def spread_a(n, cs):
             w = work[n]
-            var = stat.tile([P, 32], F32, name="var", tag="var")
+            if "var" not in w:
+                for key in ("var", "std", "sg", "q"):
+                    w[key] = stat.tile([P, 32], F32, name=key, tag=key)
             nc.vector.tensor_scalar(
-                out=var[:], in0=w["vs"][:], scalar1=1.0 / (HD - 1), scalar2=1e-30, op0=ALU.mult, op1=ALU.max
+                out=w["var"][:, cs], in0=w["vs"][:, cs], scalar1=1.0 / (HD - 1), scalar2=1e-30, op0=ALU.mult, op1=ALU.max
             )
-            w["var"] = var
 
-        def spread_b(n):
+        def spread_b(n, cs):
             w = work[n]
-            std = stat.tile([P, 32], F32, name="std", tag="std")
-            nc.scalar.activation(out=std[:], in_=w["var"][:], func=ACT.Sqrt)
-            w["std"] = std
+            nc.scalar.activation(out=w["std"][:, cs], in_=w["var"][:, cs], func=ACT.Sqrt)
 
-        def spread_c(n):
+        def spread_c(n, cs):
             w = work[n]
-            sg = stat.tile([P, 32], F32, name="sg", tag="sg")
-            nc.vector.tensor_scalar(out=sg[:], in0=w["std"][:], scalar1=1e-8, scalar2=None, op0=ALU.add)
-            q = stat.tile([P, 32], F32, name="q", tag="q")
-            nc.vector.reciprocal(out=q[:], in_=sg[:])
-            w["q"] = q
+            nc.vector.tensor_scalar(out=w["sg"][:, cs], in0=w["std"][:, cs], scalar1=1e-8, scalar2=None, op0=ALU.add)
+            nc.vector.reciprocal(out=w["q"][:, cs], in_=w["sg"][:, cs])
 
         bxks = {}
 
@@ -470,12 +470,34 @@ def tile_tttwrapper_pa_kernel(
         def unit_at(k):
             return k // 4 if (0 <= k < NSTEP and k % 4 == 0) else None
 
-        for s in range(NSTEP + 11):
+        LAST = NSTEP - 4
+
+        def target_step(k):
+            return k + 7 if k >= LAST else k + 10
+
+        def weigh_step(k):
+            return k + 7 if k >= LAST else k + 8
+
+        def spreads(s):
+            if at(s - 7) and s - 7 >= LAST:
+                return [(s - 7) // 4, slice(8 * ((s - 7) % 4), 8 * ((s - 7) % 4) + 8)]
+            if unit_at(s - 10) is not None and s - 10 < LAST:
+                return [unit_at(s - 10), slice(0, 32)]
+            return None
+
+        due = {}
+        for k in range(NSTEP):
+            due.setdefault(target_step(k), []).append(k)
+        order = [k for s in sorted(due) for k in due[s]]
+        shifted = 0
+        finished = 0
+
+        for s in range(max(due) + 1):
             if unit_at(s - 5) is not None:
                 norm_c(unit_at(s - 5))
-            if unit_at(s - 10) is not None:
-                spread_a(unit_at(s - 10))
-                spread_b(unit_at(s - 10))
+            if spreads(s):
+                spread_a(*spreads(s))
+                spread_b(*spreads(s))
             if at(s - 6):
                 run(subtract(*at(s - 6)))
             if at(s - 5):
@@ -488,20 +510,24 @@ def tile_tttwrapper_pa_kernel(
                 run(turn(1 + (s - 1) // 4, (s - 1) % 4))
             if at(s - 6):
                 mean(*at(s - 6))
-            if at(s - 9):
-                weigh(*at(s - 9))
+            for k in range(NSTEP):
+                if weigh_step(k) == s:
+                    weigh(*at(k))
             if at(s - 5):
                 keys(*at(s - 5))
-            if unit_at(s - 10) is not None:
-                spread_c(unit_at(s - 10))
-            if at(s - 10):
-                scale(*at(s - 10))
+            if spreads(s):
+                spread_c(*spreads(s))
+            for k in due.get(s, []):
+                scale(*at(k))
             if at(s - 6):
                 difference(*at(s - 6))
-            if at(s - 10):
-                target(*at(s - 10))
-            if at(s - 9):
-                shifted_keys(*at(s - 9))
+            for k in due.get(s, []) + [None]:
+                if k is not None:
+                    target(*at(k))
+                    finished += 1
+                while shifted < min(NSTEP, finished + 2) and order[shifted] + 5 < s:
+                    shifted_keys(*at(order[shifted]))
+                    shifted += 1
             if 1 <= s <= 12:
                 evacuate(1 + (s - 1) // 4, (s - 1) % 4)
             if 0 <= s + 1 < 8:
@@ -515,6 +541,10 @@ def tile_tttwrapper_pa_kernel(
                 widen(1 + s // 4, s % 4)
             if s + 1 < 4:
                 table_a(s + 1)
+            if unit_at(s - 4) is not None:
+                norm_sum(unit_at(s - 4))
+            if unit_at(s - 5) is not None:
+                mean_sum(unit_at(s - 5))
             if at(s):
                 matmuls(*at(s))
                 scalar_out(*at(s))

@@ -311,7 +311,7 @@ def tile_tttwrapper_pa_kernel(
 
         def mean_a(n):
             mv = work[n]["mv"]
-            nc.vector.tensor_scalar(out=mv[:], in0=mv[:], scalar1=1.0 / HD, scalar2=None, op0=ALU.mult)
+            nc.scalar.activation(out=mv[:], in_=mv[:], func=ACT.Copy, scale=1.0 / HD)
 
         def turn_back(n, t):
             w = work[n]
@@ -390,22 +390,16 @@ def tile_tttwrapper_pa_kernel(
                     accum_out=w["vs"][:, c : c + 1],
                 )
 
-        def spread_a(n, cs):
-            w = work[n]
-            if "var" not in w:
-                for key in ("var", "std", "sg", "q"):
-                    w[key] = stat.tile([P, 32], F32, name=key, tag=key)
-            nc.vector.tensor_scalar(
-                out=w["var"][:, cs], in0=w["vs"][:, cs], scalar1=1.0 / (HD - 1), scalar2=1e-30, op0=ALU.mult, op1=ALU.max
-            )
-
         def spread_b(n, cs):
             w = work[n]
-            nc.scalar.activation(out=w["std"][:, cs], in_=w["var"][:, cs], func=ACT.Sqrt)
+            if "std" not in w:
+                for key in ("std", "sg", "q"):
+                    w[key] = stat.tile([P, 32], F32, name=key, tag=key)
+            nc.scalar.activation(out=w["std"][:, cs], in_=w["vs"][:, cs], func=ACT.Sqrt, scale=1.0 / (HD - 1), bias=1e-30)
+            nc.scalar.activation(out=w["sg"][:, cs], in_=w["std"][:, cs], func=ACT.Identity, bias=1e-8)
 
         def spread_c(n, cs):
             w = work[n]
-            nc.vector.tensor_scalar(out=w["sg"][:, cs], in0=w["std"][:, cs], scalar1=1e-8, scalar2=None, op0=ALU.add)
             nc.vector.reciprocal(out=w["q"][:, cs], in_=w["sg"][:, cs])
 
         bxks = {}
@@ -496,7 +490,6 @@ def tile_tttwrapper_pa_kernel(
             if unit_at(s - 5) is not None:
                 norm_c(unit_at(s - 5))
             if spreads(s):
-                spread_a(*spreads(s))
                 spread_b(*spreads(s))
             if at(s - 6):
                 run(subtract(*at(s - 6)))

@@ -131,7 +131,7 @@ def tile_tttwrapper_pa_kernel(
             nc.vector.tensor_scalar(
                 out=fv[:, :, 1, :, e], in0=fcv[:, :, :, 1], scalar1=(1.0 if e == 0 else -1.0), scalar2=None, op0=ALU.mult
             )
-        tabs = [const.tile([P, 4, L], BF16, name=nm) for nm in ("cos_t", "sin_t")]
+        tab = const.tile([P, 4, 2, L], BF16, name="rope_t")
         xreps = {}
 
         def table_a(i):
@@ -147,7 +147,7 @@ def tile_tttwrapper_pa_kernel(
                 pc = pool.tile([P, L], F32, name="pc", tag=tg)
                 for t in range(4):
                     turn_op(pc[:, t * P : (t + 1) * P], xreps[(i, c)][:, t, :, :].rearrange("p h d -> p (h d)"), ident, True, True)()
-                nc.scalar.copy(out=tabs[c][:, i, :], in_=pc[:])
+                nc.scalar.copy(out=tab[:, i, c, :], in_=pc[:])
 
         table_a(0)
         table_b(0)
@@ -229,7 +229,7 @@ def tile_tttwrapper_pa_kernel(
             tok = slice(b * L, (b + 1) * L)
             c = 4 * hf + i
             if i == 0:
-                work[n] = {"a": [], "bb": [], "sq": [], "vt": [], "xk": [], "y": [], "pk": [], "pv": [], "rk": [], "v0": []}
+                work[n] = {"ab": [], "sq": [], "vt": [], "xk": [], "y": [], "pk": [], "pv": [], "rk": [], "v0": []}
             w = work[n]
             for mat, key in ((0, "pk"), (1, "pv")):
                 acc = ps_mx.tile([P, L], F32, name=key, tag=key, bufs=1)
@@ -260,12 +260,16 @@ def tile_tttwrapper_pa_kernel(
         def vector_out(n, i):
             ct = 4 * (n % 2) + i
             w = work[n]
-            for key, c in (("a", 0), ("bb", 1)):
-                prod = chan.tile([P, L], F32, name=key, tag=key)
-                nc.vector.scalar_tensor_tensor(
-                    out=prod[:], in0=w["pk"][i][:], scalar=bias_t[:, ct : ct + 1], in1=tabs[c][:, i, :], op0=ALU.add, op1=ALU.mult
-                )
-                w[key].append(prod)
+            prod = chan.tile([P, 2, L], F32, name="ab", tag="ab")
+            nc.vector.scalar_tensor_tensor(
+                out=prod[:],
+                in0=w["pk"][i][:].unsqueeze(1).to_broadcast([P, 2, L]),
+                scalar=bias_t[:, ct : ct + 1],
+                in1=tab[:, i, :, :],
+                op0=ALU.add,
+                op1=ALU.mult,
+            )
+            w["ab"].append(prod)
 
         def fold(n, key):
             w = work[n]
@@ -321,8 +325,8 @@ def tile_tttwrapper_pa_kernel(
             ops = []
             for i in range(4):
                 cs = slice(i * P, (i + 1) * P)
-                ops.append(turn_op(rk[:, cs], w["a"][i][:, ts], ident, True, False))
-                ops.append(turn_op(rk[:, cs], w["bb"][i][:, ts], pswap, False, True))
+                ops.append(turn_op(rk[:, cs], w["ab"][i][:, 0, ts], ident, True, False))
+                ops.append(turn_op(rk[:, cs], w["ab"][i][:, 1, ts], pswap, False, True))
             return ops
 
         def subtract(n, t):
@@ -491,10 +495,10 @@ def tile_tttwrapper_pa_kernel(
                 norm_c(unit_at(s - 5))
             if spreads(s):
                 spread_b(*spreads(s))
-            if at(s - 6):
-                run(subtract(*at(s - 6)))
             if at(s - 5):
                 run(turn_back(*at(s - 5)))
+            if at(s - 6):
+                run(subtract(*at(s - 6)))
             if unit_at(s - 4) is not None:
                 run(fold(unit_at(s - 4), "sq"))
             if unit_at(s - 5) is not None:

@@ -74,13 +74,18 @@ def tile_tttwrapper_pa_kernel(
 
         hbytes = {}
 
-        def load_bytes(b):
+        def load_bytes(b, pieces):
             hb = bytes_pool.tile([P, 4, D], U8, name="hbytes", tag="hbytes")
-            nc.sync.dma_start(out=hb[:], in_=hidden_states_bytes[b].rearrange("(t p) k -> p t k", p=P))
+            rows = hidden_states_bytes[b].rearrange("(t p) k -> p t k", p=P)
+            n = 4 // pieces
+            for q in range(pieces):
+                nc.sync.dma_start(out=hb[:, n * q : n * (q + 1), :], in_=rows[:, n * q : n * (q + 1), :])
             hbytes[b] = hb
 
+        sc = const.tile([P, D], F32, name="sc")
+        nc.scalar.dma_start(out=sc[:], in_=hidden_states_scale.rearrange("a b k -> (a b k)").partition_broadcast(P))
         fc = const.tile([P, 4, 64], BF16, name="fc")
-        nc.scalar.dma_start(out=fc[:], in_=freqs_cis.rearrange("(t p) j c -> p t (j c)", p=P))
+        nc.sync.dma_start(out=fc[:], in_=freqs_cis.rearrange("(t p) j c -> p t (j c)", p=P))
         brow = const.tile([P, P], BF16, name="brow")
         nc.vector.memset(brow[:], 0.0)
         for m, vec in enumerate((wk_b, wv_b)):
@@ -89,20 +94,20 @@ def tile_tttwrapper_pa_kernel(
                     out=brow[8 * m + 4 * f : 8 * m + 4 * f + 4, :].rearrange("r (h d) -> r h d", h=UH),
                     in_=vec.rearrange("(f h i d) -> f i h d", f=2, h=UH, i=4)[f],
                 )
-        sc = const.tile([P, D], F32, name="sc")
-        nc.scalar.dma_start(out=sc[:], in_=hidden_states_scale.rearrange("a b k -> (a b k)").partition_broadcast(P))
-        load_bytes(0)
+        load_bytes(0, 4)
         load_weights(0, 0)
         load_weights(1, 0)
-        w_b = const.tile([P, D], BF16, name="w_b")
-        nc.scalar.dma_start(out=w_b[:], in_=ttt_norm_weight.rearrange("h d -> (h d)").partition_broadcast(P))
-        b_b = const.tile([P, D], BF16, name="b_b")
-        nc.scalar.dma_start(out=b_b[:], in_=ttt_norm_bias.rearrange("h d -> (h d)").partition_broadcast(P))
-        load_bytes(1)
+        load_bytes(1, 1)
         load_weights(0, 1)
         load_weights(1, 1)
-        load_bytes(2)
-        load_bytes(3)
+        load_bytes(2, 1)
+        load_bytes(3, 1)
+        w_b = const.tile([P, D], BF16, name="w_b")
+        b_b = const.tile([P, D], BF16, name="b_b")
+
+        def load_norm_rows():
+            nc.scalar.dma_start(out=b_b[:], in_=ttt_norm_bias.rearrange("h d -> (h d)").partition_broadcast(P))
+            nc.scalar.dma_start(out=w_b[:], in_=ttt_norm_weight.rearrange("h d -> (h d)").partition_broadcast(P))
 
         one = const.tile([P, 1], F32, name="one")
         nc.vector.memset(one[:], 1.0)
@@ -152,12 +157,7 @@ def tile_tttwrapper_pa_kernel(
         table_a(0)
         table_b(0)
 
-        browf = const.tile([P, P], F32, name="browf")
-        nc.vector.tensor_copy(out=browf[:], in_=brow[:])
-        pb = ps_st.tile([P, P], F32, name="pb", tag="st")
-        nc.tensor.transpose(pb[:], browf[:], ident[:])
         bias_t = const.tile([P, 16], F32, name="bias_t")
-        nc.scalar.copy(out=bias_t[:], in_=pb[:, 0:16])
 
         wcodes = [codes.tile([P, 8, 2, P], U32, name="wcodes%d" % m, align_bytes=64) for m in range(2)]
         wscales = [codes.tile([P, 8, 2, P], U8, name="wscales%d" % m, align_bytes=64) for m in range(2)]
@@ -451,6 +451,11 @@ def tile_tttwrapper_pa_kernel(
         evacuate(0, 2)
         run(turn(0, 3))
         evacuate(0, 3)
+        browf = const.tile([P, P], F32, name="browf")
+        nc.vector.tensor_copy(out=browf[:], in_=brow[:])
+        pb = ps_st.tile([P, P], F32, name="pb", tag="st")
+        nc.tensor.transpose(pb[:], browf[:], ident[:])
+        nc.scalar.copy(out=bias_t[:], in_=pb[:, 0:16])
         copy_chunk(0, 0)
         quant_hidden(0, 0)
         quant_chunk(0, 0)
@@ -491,6 +496,8 @@ def tile_tttwrapper_pa_kernel(
         finished = 0
 
         for s in range(max(due) + 1):
+            if s == 1:
+                load_norm_rows()
             if unit_at(s - 5) is not None:
                 norm_c(unit_at(s - 5))
             if spreads(s):

@@ -292,20 +292,21 @@ def tile_tttwrapper_pa_kernel(
             work[n]["ss"] = head_sum(n, "sq", "ss")
 
         def norm_a(n):
-            ss = work[n]["ss"]
+            w = work[n]
+            ss = w["ss"]
             nc.vector.tensor_scalar(out=ss[:], in0=ss[:], scalar1=1e-24, scalar2=None, op0=ALU.max)
+            rho = stat.tile([P, 32], F32, name="rho", tag="rho")
+            nc.vector.reciprocal(out=rho[:], in_=ss[:])
+            w["rho"] = rho
 
         def norm_b(n):
             w = work[n]
-            rho = stat.tile([P, 32], F32, name="rho", tag="rho")
-            nc.scalar.activation(out=rho[:], in_=w["ss"][:], func=ACT.Sqrt)
-            w["rho"] = rho
+            r = stat.tile([P, 32], F32, name="r", tag="r")
+            nc.scalar.activation(out=r[:], in_=w["rho"][:], func=ACT.Sqrt)
+            w["r"] = r
 
         def norm_c(n):
             w = work[n]
-            r = stat.tile([P, 32], F32, name="r", tag="r")
-            nc.vector.reciprocal(out=r[:], in_=w["rho"][:])
-            w["r"] = r
             w["sxk"] = stat.tile([P, 32], F32, name="sxk", tag="sxk")
             w["vs"] = stat.tile([P, 32], F32, name="vs", tag="vs")
             w["negm"] = stat.tile([P, 32], F32, name="negm", tag="negm")

@@ -47,7 +47,7 @@ def tile_tttwrapper_pa_kernel(
         chan = ctx.enter_context(tc.tile_pool(name="chan", bufs=9))
         sq_pool = ctx.enter_context(tc.tile_pool(name="sq_pool", bufs=5))
         xk_pool = ctx.enter_context(tc.tile_pool(name="xk_pool", bufs=6))
-        y_pool = ctx.enter_context(tc.tile_pool(name="y_pool", bufs=7))
+        y_pool = ctx.enter_context(tc.tile_pool(name="y_pool", bufs=8))
         bxk_pool = ctx.enter_context(tc.tile_pool(name="bxk_pool", bufs=2))
         stat = ctx.enter_context(tc.tile_pool(name="stat", bufs=4))
         ps_mx = ctx.enter_context(tc.psum_pool(name="ps_mx", bufs=2))
@@ -427,6 +427,14 @@ def tile_tttwrapper_pa_kernel(
             yv = work[n]["y"][t][:].rearrange("p (h d) -> p h d", h=UH)
             nc.vector.tensor_tensor(out=yv, in0=yv, in1=by_head(n, t, "q"), op=ALU.mult)
 
+        def scale_by_head(n, t):
+            w = work[n]
+            y = w["y"][t]
+            for h in range(UH):
+                c = t * 8 + h
+                hs = slice(h * HD, (h + 1) * HD)
+                nc.scalar.activation(out=y[:, hs], in_=y[:, hs], func=ACT.Copy, scale=w["q"][:, c : c + 1])
+
         def target(n, t):
             b, hf = divmod(n, 2)
             w = work[n]
@@ -475,9 +483,12 @@ def tile_tttwrapper_pa_kernel(
             return k // 4 if (0 <= k < NSTEP and k % 4 == 0) else None
 
         LAST = NSTEP - 4
+        ON_SCALAR = NSTEP - 8
 
         def target_step(k):
-            return k + 7 if k >= LAST else k + 10
+            if k >= LAST:
+                return k + 7
+            return k + 11 if k < ON_SCALAR else k + 10
 
         def weigh_step(k):
             return k + 7 if k >= LAST else k + 8
@@ -523,7 +534,8 @@ def tile_tttwrapper_pa_kernel(
             if spreads(s):
                 spread_c(*spreads(s))
             for k in due.get(s, []):
-                scale(*at(k))
+                if k >= ON_SCALAR:
+                    scale(*at(k))
             if at(s - 6):
                 difference(*at(s - 6))
             for k in due.get(s, []) + [None]:
@@ -556,6 +568,8 @@ def tile_tttwrapper_pa_kernel(
                 vector_out(*at(s))
             if at(s - 6):
                 squares(*at(s - 6))
+            if at(s - 10) and s - 10 < ON_SCALAR:
+                scale_by_head(*at(s - 10))
             if 0 <= s + 2 < 8:
                 copy_chunk(1, s + 2)
             if s + 1 < 4:

@@ -490,6 +490,9 @@ def tile_tttwrapper_pa_kernel(
                 return k + 7
             return k + 11 if k < ON_SCALAR else k + 10
 
+        def by_scalar(k):
+            return k < ON_SCALAR and k % 2 == 0
+
         def weigh_step(k):
             return k + 7 if k >= LAST else k + 8
 
@@ -534,7 +537,7 @@ def tile_tttwrapper_pa_kernel(
             if spreads(s):
                 spread_c(*spreads(s))
             for k in due.get(s, []):
-                if k >= ON_SCALAR:
+                if not by_scalar(k):
                     scale(*at(k))
             if at(s - 6):
                 difference(*at(s - 6))
@@ -568,7 +571,7 @@ def tile_tttwrapper_pa_kernel(
                 vector_out(*at(s))
             if at(s - 6):
                 squares(*at(s - 6))
-            if at(s - 10) and s - 10 < ON_SCALAR:
+            if at(s - 10) and by_scalar(s - 10):
                 scale_by_head(*at(s - 10))
             if 0 <= s + 2 < 8:
                 copy_chunk(1, s + 2)

@@ -335,6 +335,8 @@ def tile_tttwrapper_pa_kernel(
             ts = slice(t * P, (t + 1) * P)
             v0 = ps_v0.tile([P, 512], F32, name="v0", tag="v0")
             w["v0"].append(v0)
+            if by_scalar(4 * n + t):
+                return [turn_op(v0[:, i * P : (i + 1) * P], w["vt"][i][:, ts], ident, True, True) for i in range(4)]
             ops = [
                 lambda: nc.tensor.matmul(
                     out=v0[:].rearrange("p (i h d) -> p i h d", i=4, h=UH),
@@ -374,12 +376,20 @@ def tile_tttwrapper_pa_kernel(
         def difference(n, t):
             w = work[n]
             y = y_pool.tile([P, 512], F32, name="y", tag="y")
-            nc.vector.tensor_tensor(
-                out=y[:].rearrange("p (h i d) -> p h i d", h=UH, i=4),
-                in0=w["v0"][t][:].rearrange("p (i h d) -> p h i d", i=4, h=UH),
-                in1=w["negm"][:, t * 8 : (t + 1) * 8].unsqueeze(2).unsqueeze(3).to_broadcast([P, UH, 4, CD]),
-                op=ALU.add,
-            )
+            if by_scalar(4 * n + t):
+                nc.vector.tensor_tensor(
+                    out=y[:].rearrange("p (h i d) -> p h i d", h=UH, i=4),
+                    in0=w["v0"][t][:].rearrange("p (i h d) -> p h i d", i=4, h=UH),
+                    in1=w["xk"][t][:].rearrange("p (h i d) -> p h i d", h=UH, i=4),
+                    op=ALU.subtract,
+                )
+            else:
+                nc.vector.tensor_tensor(
+                    out=y[:].rearrange("p (h i d) -> p h i d", h=UH, i=4),
+                    in0=w["v0"][t][:].rearrange("p (i h d) -> p h i d", i=4, h=UH),
+                    in1=w["negm"][:, t * 8 : (t + 1) * 8].unsqueeze(2).unsqueeze(3).to_broadcast([P, UH, 4, CD]),
+                    op=ALU.add,
+                )
             w["y"].append(y)
 
         def squares(n, t):
@@ -392,6 +402,7 @@ def tile_tttwrapper_pa_kernel(
                     out=junk[:, hs],
                     in_=w["y"][t][:, hs],
                     func=ACT.Square,
+                    bias=(w["negm"][:, c : c + 1] if by_scalar(4 * n + t) else 0.0),
                     accum_out=w["vs"][:, c : c + 1],
                 )
 
@@ -406,6 +417,9 @@ def tile_tttwrapper_pa_kernel(
         def spread_c(n, cs):
             w = work[n]
             nc.vector.reciprocal(out=w["q"][:, cs], in_=w["sg"][:, cs])
+            if by_scalar(4 * n):
+                w["nb"] = stat.tile([P, 32], F32, name="nb", tag="nb")
+                nc.vector.tensor_tensor(out=w["nb"][:], in0=w["negm"][:], in1=w["q"][:], op=ALU.mult)
 
         bxks = {}
 
@@ -433,7 +447,9 @@ def tile_tttwrapper_pa_kernel(
             for h in range(UH):
                 c = t * 8 + h
                 hs = slice(h * HD, (h + 1) * HD)
-                nc.scalar.activation(out=y[:, hs], in_=y[:, hs], func=ACT.Copy, scale=w["q"][:, c : c + 1])
+                nc.scalar.activation(
+                    out=y[:, hs], in_=y[:, hs], func=ACT.Identity, scale=w["q"][:, c : c + 1], bias=w["nb"][:, c : c + 1]
+                )
 
         def target(n, t):
             b, hf = divmod(n, 2)
@@ -494,6 +510,8 @@ def tile_tttwrapper_pa_kernel(
             return k < ON_SCALAR and k % 2 == 0
 
         def weigh_step(k):
+            if by_scalar(k):
+                return k + 11
             return k + 7 if k >= LAST else k + 8
 
         def spreads(s):

@@ -47,7 +47,7 @@ def tile_tttwrapper_pa_kernel(
         chan = ctx.enter_context(tc.tile_pool(name="chan", bufs=9))
         sq_pool = ctx.enter_context(tc.tile_pool(name="sq_pool", bufs=5))
         xk_pool = ctx.enter_context(tc.tile_pool(name="xk_pool", bufs=6))
-        y_pool = ctx.enter_context(tc.tile_pool(name="y_pool", bufs=8))
+        y_pool = ctx.enter_context(tc.tile_pool(name="y_pool", bufs=9))
         bxk_pool = ctx.enter_context(tc.tile_pool(name="bxk_pool", bufs=2))
         stat = ctx.enter_context(tc.tile_pool(name="stat", bufs=4))
         ps_mx = ctx.enter_context(tc.psum_pool(name="ps_mx", bufs=2))
@@ -394,7 +394,7 @@ def tile_tttwrapper_pa_kernel(
 
         def squares(n, t):
             w = work[n]
-            junk = stat.tile([P, UH * HD], BF16, name="junk", tag="junk")
+            junk = stat.tile([P, UH * HD], BF16, name="junk", tag="junk", bufs=1)
             for h in range(UH):
                 c = t * 8 + h
                 hs = slice(h * HD, (h + 1) * HD)
@@ -504,10 +504,10 @@ def tile_tttwrapper_pa_kernel(
         def target_step(k):
             if k >= LAST:
                 return k + 7
-            return k + 11 if k < ON_SCALAR else k + 10
+            return k + 12 if k < ON_SCALAR else k + 10
 
         def by_scalar(k):
-            return k < ON_SCALAR and k % 2 == 0
+            return k < ON_SCALAR
 
         def weigh_step(k):
             if by_scalar(k):
@@ -547,7 +547,7 @@ def tile_tttwrapper_pa_kernel(
                 run(turn(1 + (s - 1) // 4, (s - 1) % 4))
             if at(s - 6):
                 mean(*at(s - 6))
-            for k in range(NSTEP):
+            for k in range(ON_SCALAR, NSTEP):
                 if weigh_step(k) == s:
                     weigh(*at(k))
             if at(s - 5):
@@ -566,6 +566,8 @@ def tile_tttwrapper_pa_kernel(
                 while shifted < min(NSTEP, finished + 2) and order[shifted] + 5 < s:
                     shifted_keys(*at(order[shifted]))
                     shifted += 1
+            if at(s - 11) and by_scalar(s - 11):
+                weigh(*at(s - 11))
             if 1 <= s <= 12:
                 evacuate(1 + (s - 1) // 4, (s - 1) % 4)
             if 0 <= s + 1 < 8:

from contextlib import ExitStack

import concourse.mybir as mybir
from concourse.masks import make_identity

F32 = mybir.dt.float32
BF16 = mybir.dt.bfloat16
U8 = mybir.dt.uint8
U32 = mybir.dt.uint32
FP8 = mybir.dt.float8_e4m3fn
FP8X4 = mybir.dt.float8_e4m3fn_x4
ALU = mybir.AluOpType
ACT = mybir.ActivationFunctionType
AX = mybir.AxisListType

B, L, D, H, HD = 4, 512, 1024, 16, 64
P = 128
UH = 8
CD = 16
FLOPS = 2 * (B * L) * D * (2 * D)


def tile_tttwrapper_pa_kernel(
    tc,
    hidden_states_bytes,
    hidden_states_scale,
    freqs_cis,
    wk_w,
    wk_b,
    wv_w,
    wv_b,
    ttt_norm_weight,
    ttt_norm_bias,
    out_0,
    out_1,
):
    nc = tc.nc
    with ExitStack() as ctx:
        const = ctx.enter_context(tc.tile_pool(name="const", bufs=1))
        codes = ctx.enter_context(tc.tile_pool(name="codes", bufs=1))
        bytes_pool = ctx.enter_context(tc.tile_pool(name="bytes_pool", bufs=2))
        wraw_pool = ctx.enter_context(tc.tile_pool(name="wraw_pool", bufs=2))
        wgrp_pool = ctx.enter_context(tc.tile_pool(name="wgrp_pool", bufs=4))
        xb_pool = ctx.enter_context(tc.tile_pool(name="xb_pool", bufs=2))
        hgrp_pool = ctx.enter_context(tc.tile_pool(name="hgrp_pool", bufs=2))
        xrep_pool = ctx.enter_context(tc.tile_pool(name="xrep_pool", bufs=2))
        chan = ctx.enter_context(tc.tile_pool(name="chan", bufs=9))
        sq_pool = ctx.enter_context(tc.tile_pool(name="sq_pool", bufs=5))
        xk_pool = ctx.enter_context(tc.tile_pool(name="xk_pool", bufs=6))
        y_pool = ctx.enter_context(tc.tile_pool(name="y_pool", bufs=9))
        bxk_pool = ctx.enter_context(tc.tile_pool(name="bxk_pool", bufs=2))
        stat = ctx.enter_context(tc.tile_pool(name="stat", bufs=4))
        ps_mx = ctx.enter_context(tc.psum_pool(name="ps_mx", bufs=2))
        ps_rk = ctx.enter_context(tc.psum_pool(name="ps_rk", bufs=2))
        ps_v0 = ctx.enter_context(tc.psum_pool(name="ps_v0", bufs=2))
        ps_st = ctx.enter_context(tc.psum_pool(name="ps_st", bufs=1))
        ps_xt = ctx.enter_context(tc.psum_pool(name="ps_xt", bufs=1))
        ctx.enter_context(tc.manual_schedule())

        weights = (wk_w, wv_w)

        wraw = {}

        def load_weights(mat, hf):
            raw = wraw_pool.tile([P, 2, 4, 512], BF16, name="wraw%d" % mat, tag="wraw%d" % mat)
            for g in range(2):
                nc.sync.dma_start(
                    out=raw[:, g, :, :],
                    in_=weights[mat][512 * g : 512 * (g + 1), 512 * hf : 512 * (hf + 1)].rearrange(
                        "(p j) n -> p j n", j=4
                    ),
                )
            wraw[(mat, hf)] = raw

        hbytes = {}

        def load_bytes(b, pieces):
            hb = bytes_pool.tile([P, 4, D], U8, name="hbytes", tag="hbytes")
            rows = hidden_states_bytes[b].rearrange("(t p) k -> p t k", p=P)
            n = 4 // pieces
            for q in range(pieces):
                nc.sync.dma_start(out=hb[:, n * q : n * (q + 1), :], in_=rows[:, n * q : n * (q + 1), :])
            hbytes[b] = hb

        sc = const.tile([P, D], F32, name="sc")
        nc.scalar.dma_start(out=sc[:], in_=hidden_states_scale.rearrange("a b k -> (a b k)").partition_broadcast(P))
        fc = const.tile([P, 4, 64], BF16, name="fc")
        nc.sync.dma_start(out=fc[:], in_=freqs_cis.rearrange("(t p) j c -> p t (j c)", p=P))
        brow = const.tile([P, P], BF16, name="brow")
        nc.vector.memset(brow[:], 0.0)
        for m, vec in enumerate((wk_b, wv_b)):
            for f in range(2):
                nc.scalar.dma_start(
                    out=brow[8 * m + 4 * f : 8 * m + 4 * f + 4, :].rearrange("r (h d) -> r h d", h=UH),
                    in_=vec.rearrange("(f h i d) -> f i h d", f=2, h=UH, i=4)[f],
                )
        load_bytes(0, 4)
        load_weights(0, 0)
        load_weights(1, 0)
        load_bytes(1, 1)
        load_weights(0, 1)
        load_weights(1, 1)
        load_bytes(2, 1)
        load_bytes(3, 1)
        w_b = const.tile([P, D], BF16, name="w_b")
        b_b = const.tile([P, D], BF16, name="b_b")

        def load_norm_rows():
            nc.scalar.dma_start(out=b_b[:], in_=ttt_norm_bias.rearrange("h d -> (h d)").partition_broadcast(P))
            nc.scalar.dma_start(out=w_b[:], in_=ttt_norm_weight.rearrange("h d -> (h d)").partition_broadcast(P))

        one = const.tile([P, 1], F32, name="one")
        nc.vector.memset(one[:], 1.0)
        one2 = const.tile([P, 1], F32, name="one2")
        nc.scalar.activation(out=one2[:], in_=one[:], func=ACT.Sqrt)

        ident = const.tile([P, P], F32, name="ident")
        make_identity(nc, ident[:])
        pswap = const.tile([P, P], F32, name="pswap")
        iv = ident[:].rearrange("p (j e) -> p j e", e=2)
        sv = pswap[:].rearrange("p (j e) -> p j e", e=2)
        nc.gpsimd.tensor_copy(out=sv[:, :, 0:1], in_=iv[:, :, 1:2])
        nc.gpsimd.tensor_copy(out=sv[:, :, 1:2], in_=iv[:, :, 0:1])

        negi = const.tile([P, P], F32, name="negi")
        nc.gpsimd.tensor_scalar(out=negi[:], in0=ident[:], scalar1=-1.0, scalar2=0.0, op0=ALU.mult, op1=ALU.add)

        def turn_op(dst, src, perm, first, last):
            return lambda: nc.tensor.matmul(out=dst, lhsT=src, rhs=perm[:], is_transpose=True, start=first, stop=last)

        ftok = const.tile([P, 4, 2, HD], F32, name="ftok")
        fcv = fc[:].rearrange("p t (j c) -> p t j c", c=2)
        fv = ftok[:].rearrange("p t c (j e) -> p t c j e", e=2)
        for e in range(2):
            nc.vector.tensor_copy(out=fv[:, :, 0, :, e], in_=fcv[:, :, :, 0])
            nc.vector.tensor_scalar(
                out=fv[:, :, 1, :, e], in0=fcv[:, :, :, 1], scalar1=(1.0 if e == 0 else -1.0), scalar2=None, op0=ALU.mult
            )
        tab = const.tile([P, 4, 2, L], BF16, name="rope_t")
        xreps = {}

        def table_a(i):
            for c in range(2):
                xrep = xrep_pool.tile([P, 4, UH, CD], F32, name="xrep", tag="xrep")
                nc.vector.tensor_copy(
                    out=xrep[:], in_=ftok[:, :, c, CD * i : CD * (i + 1)].unsqueeze(2).to_broadcast([P, 4, UH, CD])
                )
                xreps[(i, c)] = xrep

        def table_b(i):
            for c, pool, tg in ((0, ps_rk, "rk"), (1, ps_v0, "v0")):
                pc = pool.tile([P, L], F32, name="pc", tag=tg)
                for t in range(4):
                    turn_op(pc[:, t * P : (t + 1) * P], xreps[(i, c)][:, t, :, :].rearrange("p h d -> p (h d)"), ident, True, True)()
                nc.scalar.copy(out=tab[:, i, c, :], in_=pc[:])

        table_a(0)
        table_b(0)

        bias_t = const.tile([P, 16], F32, name="bias_t")

        wcodes = [codes.tile([P, 8, 2, P], U32, name="wcodes%d" % m, align_bytes=64) for m in range(2)]
        wscales = [codes.tile([P, 8, 2, P], U8, name="wscales%d" % m, align_bytes=64) for m in range(2)]
        hcodes = codes.tile([P, 2, B * L], U32, name="hcodes", align_bytes=64)
        hscales = codes.tile([P, 2, B * L], U8, name="hscales", align_bytes=64)

        wgrp = {}

        def copy_chunk(mat, c):
            hf, i = divmod(c, 4)
            grp = wgrp_pool.tile([P, 2, P, 4], BF16, name="wgrp", tag="wgrp", align_bytes=64)
            for g in range(2):
                src = wraw[(mat, hf)][:, g, :, :].rearrange("p j (h i d) -> p i h d j", h=UH, i=4)[:, i]
                dst = grp[:, g, :, :].rearrange("p (h d) j -> p h d j", h=UH)
                if mat == 0:
                    nc.vector.tensor_copy(out=dst, in_=src)
                else:
                    nc.scalar.copy(out=dst, in_=src)
            wgrp[(mat, c)] = grp

        def quant_chunk(mat, c):
            nc.vector.quantize_mx(
                out=wcodes[mat][:, c, :, :].rearrange("p g n -> p (g n)").bitcast(FP8X4),
                scales=wscales[mat][:, c, :, :].rearrange("p g n -> p (g n)"),
                in_=wgrp[(mat, c)][:].rearrange("p g n j -> p (g n j)"),
            )

        hgrp = {}
        xbs = {}

        def widen(b, t):
            if t == 0:
                hgrp[b] = hgrp_pool.tile([P, 2, L, 4], BF16, name="hgrp", tag="hgrp", align_bytes=64)
            xb = xb_pool.tile([P, D], BF16, name="xb", tag="xb", align_bytes=64)
            nc.vector.tensor_tensor(out=xb[:], in0=hbytes[b][:, t, :].bitcast(FP8), in1=sc[:], op=ALU.mult)
            xbs[(b, t)] = xb

        xts = {}

        def turn(b, t):
            words = xbs[(b, t)][:].bitcast(F32)
            xt = ps_xt.tile([P, 2, 2, P], F32, name="xt", tag="xt")
            xts[(b, t)] = xt
            return [
                turn_op(xt[:, g, u, :], words[:, 256 * g + u : 256 * (g + 1) : 2], ident, True, True)
                for g in range(2)
                for u in range(2)
            ]

        def evacuate(b, t):
            nc.scalar.copy(
                out=hgrp[b][:].bitcast(F32)[:, :, t * P : (t + 1) * P, :],
                in_=xts[(b, t)][:].rearrange("p g u r -> p g r u"),
            )

        def quant_hidden(b, half):
            for g in range(2):
                tok = slice(b * L + half * 256, b * L + (half + 1) * 256)
                nc.vector.quantize_mx(
                    out=hcodes[:, g, tok].bitcast(FP8X4),
                    scales=hscales[:, g, tok],
                    in_=hgrp[b][:, g, half * 256 : (half + 1) * 256, :].rearrange("p r j -> p (r j)"),
                )

        work = {}

        def matmuls(n, i):
            b, hf = divmod(n, 2)
            tok = slice(b * L, (b + 1) * L)
            c = 4 * hf + i
            if i == 0:
                work[n] = {"ab": [], "sq": [], "vt": [], "xk": [], "y": [], "pk": [], "pv": [], "rk": [], "v0": []}
            w = work[n]
            for mat, key in ((0, "pk"), (1, "pv")):
                acc = ps_mx.tile([P, L], F32, name=key, tag=key, bufs=1)
                for g in range(2):
                    nc.tensor.matmul_mx(
                        out=acc[:],
                        lhsT=wcodes[mat][:, c, g, :].bitcast(FP8X4),
                        lhsT_scale=wscales[mat][:, c, g, :],
                        rhs=hcodes[:, g, tok].bitcast(FP8X4),
                        rhs_scale=hscales[:, g, tok],
                        start=(g == 0),
                        stop=(g == 1),
                    )
                w[key].append(acc)

        def scalar_out(n, i):
            ct = 4 * (n % 2) + i
            w = work[n]
            sq = sq_pool.tile([P, L], F32, name="sq", tag="sq")
            nc.scalar.activation(out=sq[:], in_=w["pk"][i][:], func=ACT.Square, bias=bias_t[:, ct : ct + 1], scale=1.0)
            vt = chan.tile([P, L], F32, name="vt", tag="vt")
            nc.scalar.activation(
                out=vt[:], in_=w["pv"][i][:], func=ACT.Identity, bias=bias_t[:, 8 + ct : 9 + ct], scale=1.0
            )
            w["sq"].append(sq)
            w["vt"].append(vt)

        def vector_out(n, i):
            ct = 4 * (n % 2) + i
            w = work[n]
            prod = chan.tile([P, 2, L], F32, name="ab", tag="ab")
            nc.vector.scalar_tensor_tensor(
                out=prod[:],
                in0=w["pk"][i][:].unsqueeze(1).to_broadcast([P, 2, L]),
                scalar=bias_t[:, ct : ct + 1],
                in1=tab[:, i, :, :],
                op0=ALU.add,
                op1=ALU.mult,
            )
            w["ab"].append(prod)

        def fold(n, key):
            w = work[n]
            st = ps_st.tile([P, 4 * P], F32, name="st", tag="st")
            w["st" + key] = st
            return [
                turn_op(st[:, t * P : (t + 1) * P], w[key][i][:, t * P : (t + 1) * P], ident, i == 0, i == 3)
                for t in range(4)
                for i in range(4)
            ]

        def head_sum(n, key, name):
            out = stat.tile([P, 32], F32, name=name, tag=name)
            nc.vector.tensor_reduce(
                out=out[:], in_=work[n]["st" + key][:].rearrange("p (c d) -> p c d", d=CD), axis=AX.X, op=ALU.add
            )
            return out

        def norm_sum(n):
            work[n]["ss"] = head_sum(n, "sq", "ss")

        def norm_a(n):
            w = work[n]
            ss = w["ss"]
            nc.vector.tensor_scalar(out=ss[:], in0=ss[:], scalar1=1e-24, scalar2=None, op0=ALU.max)
            rho = stat.tile([P, 32], F32, name="rho", tag="rho")
            nc.vector.reciprocal(out=rho[:], in_=ss[:])
            w["rho"] = rho

        def norm_b(n):
            w = work[n]
            r = stat.tile([P, 32], F32, name="r", tag="r")
            nc.scalar.activation(out=r[:], in_=w["rho"][:], func=ACT.Sqrt)
            w["r"] = r

        def norm_c(n):
            w = work[n]
            w["sxk"] = stat.tile([P, 32], F32, name="sxk", tag="sxk")
            w["vs"] = stat.tile([P, 32], F32, name="vs", tag="vs")
            w["negm"] = stat.tile([P, 32], F32, name="negm", tag="negm")

        def mean_sum(n):
            work[n]["mv"] = head_sum(n, "vt", "mv")

        def mean_a(n):
            mv = work[n]["mv"]
            nc.scalar.activation(out=mv[:], in_=mv[:], func=ACT.Copy, scale=1.0 / HD)

        def turn_back(n, t):
            w = work[n]
            ts = slice(t * P, (t + 1) * P)
            rk = ps_rk.tile([P, 512], F32, name="rk", tag="rk")
            w["rk"].append(rk)
            ops = []
            for i in range(4):
                cs = slice(i * P, (i + 1) * P)
                ops.append(turn_op(rk[:, cs], w["ab"][i][:, 0, ts], ident, True, False))
                ops.append(turn_op(rk[:, cs], w["ab"][i][:, 1, ts], pswap, False, True))
            return ops

        def subtract(n, t):
            w = work[n]
            ts = slice(t * P, (t + 1) * P)
            v0 = ps_v0.tile([P, 512], F32, name="v0", tag="v0")
            w["v0"].append(v0)
            if by_scalar(4 * n + t):
                return [turn_op(v0[:, i * P : (i + 1) * P], w["vt"][i][:, ts], ident, True, True) for i in range(4)]
            ops = [
                lambda: nc.tensor.matmul(
                    out=v0[:].rearrange("p (i h d) -> p i h d", i=4, h=UH),
                    lhsT=negi[:],
                    rhs=w["xk"][t][:].rearrange("p (h i d) -> p i h d", h=UH, i=4),
                    start=True,
                    stop=False,
                )
            ]
            for i in range(4):
                ops.append(turn_op(v0[:, i * P : (i + 1) * P], w["vt"][i][:, ts], ident, False, i == 3))
            return ops

        def keys(n, t):
            b, hf = divmod(n, 2)
            w = work[n]
            rkv = w["rk"][t][:].rearrange("p (i h d) -> p h i d", i=4, h=UH)
            xk = xk_pool.tile([P, 512], F32, name="xk", tag="xk")
            xkv = xk[:].rearrange("p (h i d) -> p h i d", h=UH, i=4)
            for h in range(UH):
                c = t * 8 + h
                nc.scalar.activation(
                    out=xkv[:, h], in_=rkv[:, h], func=ACT.Copy, scale=w["r"][:, c : c + 1], accum_out=w["sxk"][:, c : c + 1]
                )
            nc.sync.dma_start(
                out=out_0[b, t * P : (t + 1) * P, 8 * hf : 8 * hf + 8, :].rearrange("l h d -> l (h d)"), in_=xk[:]
            )
            w["xk"].append(xk)

        def mean(n, t):
            w = work[n]
            cs = slice(t * 8, (t + 1) * 8)
            nc.vector.scalar_tensor_tensor(
                out=w["negm"][:, cs], in0=w["sxk"][:, cs], scalar=1.0 / HD, in1=w["mv"][:, cs], op0=ALU.mult, op1=ALU.subtract
            )

        def difference(n, t):
            w = work[n]
            y = y_pool.tile([P, 512], F32, name="y", tag="y")
            if by_scalar(4 * n + t):
                nc.vector.tensor_tensor(
                    out=y[:].rearrange("p (h i d) -> p h i d", h=UH, i=4),
                    in0=w["v0"][t][:].rearrange("p (i h d) -> p h i d", i=4, h=UH),
                    in1=w["xk"][t][:].rearrange("p (h i d) -> p h i d", h=UH, i=4),
                    op=ALU.subtract,
                )
            else:
                nc.vector.tensor_tensor(
                    out=y[:].rearrange("p (h i d) -> p h i d", h=UH, i=4),
                    in0=w["v0"][t][:].rearrange("p (i h d) -> p h i d", i=4, h=UH),
                    in1=w["negm"][:, t * 8 : (t + 1) * 8].unsqueeze(2).unsqueeze(3).to_broadcast([P, UH, 4, CD]),
                    op=ALU.add,
                )
            w["y"].append(y)

        def squares(n, t):
            w = work[n]
            junk = stat.tile([P, UH * HD], BF16, name="junk", tag="junk", bufs=1)
            for h in range(UH):
                c = t * 8 + h
                hs = slice(h * HD, (h + 1) * HD)
                nc.scalar.activation(
                    out=junk[:, hs],
                    in_=w["y"][t][:, hs],
                    func=ACT.Square,
                    bias=(w["negm"][:, c : c + 1] if by_scalar(4 * n + t) else 0.0),
                    accum_out=w["vs"][:, c : c + 1],
                )

        def spread_b(n, cs):
            w = work[n]
            if "std" not in w:
                for key in ("std", "sg", "q"):
                    w[key] = stat.tile([P, 32], F32, name=key, tag=key)
            nc.scalar.activation(out=w["std"][:, cs], in_=w["vs"][:, cs], func=ACT.Sqrt, scale=1.0 / (HD - 1), bias=1e-30)
            nc.scalar.activation(out=w["sg"][:, cs], in_=w["std"][:, cs], func=ACT.Identity, bias=1e-8)

        def spread_c(n, cs):
            w = work[n]
            nc.vector.reciprocal(out=w["q"][:, cs], in_=w["sg"][:, cs])
            if by_scalar(4 * n):
                w["nb"] = stat.tile([P, 32], F32, name="nb", tag="nb")
                nc.vector.tensor_tensor(out=w["nb"][:], in0=w["negm"][:], in1=w["q"][:], op=ALU.mult)

        bxks = {}

        def shifted_keys(n, t):
            hf = n % 2
            bxk = bxk_pool.tile([P, 512], F32, name="bxk", tag="bxk")
            nc.gpsimd.tensor_tensor(out=bxk[:], in0=work[n]["xk"][t][:], in1=b_b[:, 512 * hf : 512 * (hf + 1)], op=ALU.add)
            bxks[(n, t)] = bxk

        def by_head(n, t, key):
            return work[n][key][:, t * 8 : (t + 1) * 8].unsqueeze(2).to_broadcast([P, UH, HD])

        def weigh(n, t):
            hf = n % 2
            y = work[n]["y"][t]
            nc.vector.tensor_tensor(out=y[:], in0=y[:], in1=w_b[:, 512 * hf : 512 * (hf + 1)], op=ALU.mult)

        def scale(n, t):
            yv = work[n]["y"][t][:].rearrange("p (h d) -> p h d", h=UH)
            nc.vector.tensor_tensor(out=yv, in0=yv, in1=by_head(n, t, "q"), op=ALU.mult)

        def scale_by_head(n, t):
            w = work[n]
            y = w["y"][t]
            for h in range(UH):
                c = t * 8 + h
                hs = slice(h * HD, (h + 1) * HD)
                nc.scalar.activation(
                    out=y[:, hs], in_=y[:, hs], func=ACT.Identity, scale=w["q"][:, c : c + 1], bias=w["nb"][:, c : c + 1]
                )

        def target(n, t):
            b, hf = divmod(n, 2)
            w = work[n]
            y = w["y"][t]
            nc.vector.tensor_tensor(out=y[:], in0=y[:], in1=bxks[(n, t)][:], op=ALU.add)
            nc.sync.dma_start(
                out=out_1[b, t * P : (t + 1) * P, 8 * hf : 8 * hf + 8, :].rearrange("l h d -> l (h d)"), in_=y[:]
            )

        def run(ops):
            for op in ops:
                op()

        widen(0, 0)
        widen(0, 1)
        run(turn(0, 0))
        evacuate(0, 0)
        widen(0, 2)
        run(turn(0, 1))
        evacuate(0, 1)
        widen(0, 3)
        run(turn(0, 2))
        evacuate(0, 2)
        run(turn(0, 3))
        evacuate(0, 3)
        browf = const.tile([P, P], F32, name="browf")
        nc.vector.tensor_copy(out=browf[:], in_=brow[:])
        pb = ps_st.tile([P, P], F32, name="pb", tag="st")
        nc.tensor.transpose(pb[:], browf[:], ident[:])
        nc.scalar.copy(out=bias_t[:], in_=pb[:, 0:16])
        copy_chunk(0, 0)
        quant_hidden(0, 0)
        quant_chunk(0, 0)
        copy_chunk(0, 1)
        quant_hidden(0, 1)
        copy_chunk(1, 0)
        copy_chunk(1, 1)
        quant_chunk(1, 0)

        NSTEP = 32

        def at(k):
            return divmod(k, 4) if 0 <= k < NSTEP else None

        def unit_at(k):
            return k // 4 if (0 <= k < NSTEP and k % 4 == 0) else None

        LAST = NSTEP - 4
        ON_SCALAR = NSTEP - 8

        def target_step(k):
            if k >= LAST:
                return k + 7
            return k + 12 if k < ON_SCALAR else k + 10

        def by_scalar(k):
            return k < ON_SCALAR

        def weigh_step(k):
            if by_scalar(k):
                return k + 11
            return k + 7 if k >= LAST else k + 8

        def spreads(s):
            if at(s - 7) and s - 7 >= LAST:
                return [(s - 7) // 4, slice(8 * ((s - 7) % 4), 8 * ((s - 7) % 4) + 8)]
            if unit_at(s - 10) is not None and s - 10 < LAST:
                return [unit_at(s - 10), slice(0, 32)]
            return None

        due = {}
        for k in range(NSTEP):
            due.setdefault(target_step(k), []).append(k)
        order = [k for s in sorted(due) for k in due[s]]
        shifted = 0
        finished = 0

        for s in range(max(due) + 1):
            if s == 1:
                load_norm_rows()
            if unit_at(s - 5) is not None:
                norm_c(unit_at(s - 5))
            if spreads(s):
                spread_b(*spreads(s))
            if at(s - 5):
                run(turn_back(*at(s - 5)))
            if at(s - 6):
                run(subtract(*at(s - 6)))
            if unit_at(s - 4) is not None:
                run(fold(unit_at(s - 4), "sq"))
            if unit_at(s - 5) is not None:
                run(fold(unit_at(s - 5), "vt"))
            if 1 <= s <= 12:
                run(turn(1 + (s - 1) // 4, (s - 1) % 4))
            if at(s - 6):
                mean(*at(s - 6))
            for k in range(ON_SCALAR, NSTEP):
                if weigh_step(k) == s:
                    weigh(*at(k))
            if at(s - 5):
                keys(*at(s - 5))
            if spreads(s):
                spread_c(*spreads(s))
            for k in due.get(s, []):
                if not by_scalar(k):
                    scale(*at(k))
            if at(s - 6):
                difference(*at(s - 6))
            for k in due.get(s, []) + [None]:
                if k is not None:
                    target(*at(k))
                    finished += 1
                while shifted < min(NSTEP, finished + 2) and order[shifted] + 5 < s:
                    shifted_keys(*at(order[shifted]))
                    shifted += 1
            if at(s - 11) and by_scalar(s - 11):
                weigh(*at(s - 11))
            if 1 <= s <= 12:
                evacuate(1 + (s - 1) // 4, (s - 1) % 4)
            if 0 <= s + 1 < 8:
                quant_chunk(0, s + 1)
                quant_chunk(1, s + 1)
            if 0 <= s + 2 < 8:
                copy_chunk(0, s + 2)
            if 2 <= s <= 13 and s % 2 == 1:
                quant_hidden(1 + (s - 2) // 4, ((s - 2) % 4) // 2)
            if 0 <= s <= 11:
                widen(1 + s // 4, s % 4)
            if s + 1 < 4:
                table_a(s + 1)
            if unit_at(s - 4) is not None:
                norm_sum(unit_at(s - 4))
            if unit_at(s - 5) is not None:
                mean_sum(unit_at(s - 5))
            if at(s):
                matmuls(*at(s))
                scalar_out(*at(s))
                vector_out(*at(s))
            if at(s - 6):
                squares(*at(s - 6))
            if at(s - 10) and by_scalar(s - 10):
                scale_by_head(*at(s - 10))
            if 0 <= s + 2 < 8:
                copy_chunk(1, s + 2)
            if s + 1 < 4:
                table_b(s + 1)
            if unit_at(s - 4) is not None:
                norm_a(unit_at(s - 4))
                norm_b(unit_at(s - 4))
            if unit_at(s - 5) is not None:
                mean_a(unit_at(s - 5))
